import numpy as np
import ml_dtypes


def mxq(x, axis, fmt="e4m3"):
    dtype, down = {"e4m3": (ml_dtypes.float8_e4m3fn, 7), "e5m2": (ml_dtypes.float8_e5m2, 14)}[fmt]
    v = np.moveaxis(np.asarray(x, np.float32).astype(ml_dtypes.bfloat16).astype(np.float64), axis, -1)
    blocks = v.reshape(v.shape[:-1] + (-1, 32))
    amax = np.abs(blocks).max(-1, keepdims=True)
    byte = np.maximum(np.where(amax > 0, np.frexp(amax)[1] - 1 + 127, 0) - down, 1)
    scale = np.exp2(byte - 127.0)
    codes = (blocks / scale).astype(np.float32).astype(dtype).astype(np.float64)
    return np.moveaxis((codes * scale).reshape(v.shape), -1, axis)


WIDE = False


def mx_kscale(k):
    if not WIDE:
        return np.ones(k)
    levels = np.array([10, -10, 5, -5, 0])
    a = np.random.permutation(np.resize(levels, k // 512 * 4)).reshape(k // 512, 4)
    idx = np.arange(k)
    return np.exp2(a[idx // 512, idx % 128 // 32])


BF16 = ml_dtypes.bfloat16


def bf(x):
    return np.asarray(x, np.float32).astype(BF16)


def f64(x):
    return np.asarray(x).astype(np.float64)


B, T, N, D, L = 4, 8, 128, 1024, 512


def setup_inputs():
    s, r = mx_kscale(D), mx_kscale(L)
    x = np.random.standard_normal((B, T, N, D)) + 0.5 * np.random.standard_normal(D)
    return {"x": bf(x * s),
            "Wtheta": bf(np.random.standard_normal((L, D)) / np.sqrt(D) / s * r[:, None]),
            "Wphi": bf(np.random.standard_normal((L, D)) / np.sqrt(D) / s / r[:, None])}


def reference(x, Wtheta, Wphi):
    xq = mxq(f64(x), 3, "e4m3")
    th = xq @ mxq(f64(Wtheta), 1, "e4m3").T
    ph = xq @ mxq(f64(Wphi), 1, "e4m3").T
    thq, phq = mxq(th, 3, "e4m3"), mxq(ph, 3, "e4m3")
    sw = (thq @ phq.transpose(0, 1, 3, 2)) / N
    tw = (thq.transpose(0, 2, 1, 3) @ phq.transpose(0, 2, 3, 1)).transpose(0, 2, 1, 3) / T
    return sw, tw

@@ -1,0 +1,236 @@
+from contextlib import ExitStack
+
+import concourse.masks as masks
+import concourse.mybir as mybir
+
+F32 = mybir.dt.float32
+BF16 = mybir.dt.bfloat16
+U32 = mybir.dt.uint32
+I32 = mybir.dt.int32
+U8 = mybir.dt.uint8
+FP8X4 = mybir.dt.float8_e4m3fn_x4
+ALU = mybir.AluOpType
+
+P = 128
+B, T, N, D, L = 4, 8, 128, 1024, 512
+FRAMES = B * T
+PAIRS = FRAMES // 2
+FLOPS = 2 * 2 * FRAMES * N * D * L + 2 * FRAMES * N * N * L + 2 * B * N * T * T * L
+
+
+def tile_higcin_volleyball_pa_t_kernel(tc, x, Wtheta, Wphi, out_0, out_1):
+    nc = tc.nc
+    with ExitStack() as ctx:
+        keep = ctx.enter_context(tc.tile_pool(name="keep", bufs=1))
+        psum = ctx.enter_context(tc.psum_pool(name="psum", bufs=1))
+        ctx.enter_context(tc.manual_schedule())
+
+        banks = [psum.tile([P, 4, P], F32, name="bank%d" % k) for k in range(8)]
+
+        w_raw = [[keep.tile([P, 2, D], BF16, name="w_raw%d%d" % (z, h)) for h in range(2)] for z in range(2)]
+        chunks = [(0, 2), (2, 2)] + [(f, 4) for f in range(4, FRAMES, 4)]
+        x_raw = [keep.tile([P, n, D], BF16, name="x_raw%d" % f0) for (f0, n) in chunks]
+        frame_src = {}
+        for k, (f0, n) in enumerate(chunks):
+            for i in range(n):
+                frame_src[f0 + i] = (k, i)
+
+        ident = keep.tile([P, P], F32, name="ident")
+        m16raw = keep.tile([P, 16], F32, name="m16raw")
+        m16 = keep.tile([P, 16], F32, name="m16")
+
+        w_grp = [[keep.tile([P, 2, 2, P, 4], BF16, name="w_grp%d%d" % (z, h), align_bytes=64) for h in range(2)]
+                 for z in range(2)]
+        w_codes = [keep.tile([P, 8 * P], U32, name="w_codes%d" % z, align_bytes=64) for z in range(2)]
+        w_scales = [keep.tile([P, 8 * P], U8, name="w_scales%d" % z, align_bytes=64) for z in range(2)]
+
+        x_grp = [keep.tile([P, 2, 2, P, 4], BF16, name="x_grp%d" % k, align_bytes=64) for k in range(2)]
+        x_codes = [keep.tile([P, 4 * P], U32, name="x_codes%d" % k, align_bytes=64) for k in range(2)]
+        x_scales = [keep.tile([P, 4 * P], U8, name="x_scales%d" % k, align_bytes=64) for k in range(2)]
+
+        h_grp = [keep.tile([P, 2, 2, P, 4], BF16, name="h_grp%d" % k, align_bytes=64) for k in range(2)]
+        ha_codes = [keep.tile([P, 4 * P], U32, name="ha_codes%d" % k, align_bytes=64) for k in range(4)]
+        ha_scales = [keep.tile([P, 4 * P], U8, name="ha_scales%d" % k, align_bytes=64) for k in range(4)]
+        hb_codes = [keep.tile([P, 16 * P], U32, name="hb_codes%d" % k, align_bytes=64) for k in range(2)]
+        hb_scales = [keep.tile([P, 16 * P], U8, name="hb_scales%d" % k, align_bytes=64) for k in range(2)]
+
+        sw_sb = [keep.tile([P, 4, P], F32, name="sw_sb%d" % k) for k in range(3)]
+        tw_tmp = [keep.tile([P, 32, 16], F32, name="tw_tmp%d" % k) for k in range(2)]
+        tw_res = keep.tile([P, B, 64], F32, name="tw_res")
+
+        xf = x.rearrange("b t j d -> j (b t) d")
+        swf = out_0.rearrange("b t j k -> j (b t) k")
+        w_dram = [w.rearrange("(p u) d -> p u d", u=4) for w in (Wtheta, Wphi)]
+
+        def load_w(z):
+            for h in range(2):
+                nc.sync.dma_start(out=w_raw[z][h][:], in_=w_dram[z][:, 2 * h:2 * h + 2, :])
+
+        def load_x(k):
+            f0, n = chunks[k]
+            nc.sync.dma_start(out=x_raw[k][:], in_=xf[:, f0:f0 + n, :])
+
+        load_w(0)
+        load_x(0)
+        load_w(1)
+        for k in range(1, len(chunks)):
+            load_x(k)
+
+        masks.make_identity(nc, ident[:])
+        for k in range(4):
+            nc.vector.memset(ha_scales[k][:].bitcast(I32), 0)
+        nc.vector.tensor_reduce(out=m16raw[:], in_=ident[:].rearrange("p (t j) -> p j t", j=16),
+                                axis=mybir.AxisListType.X, op=ALU.add)
+        nc.vector.tensor_scalar_mul(out=m16[:], in0=m16raw[:], scalar1=1.0 / T)
+
+        def transposes(bank, src):
+            words = src.bitcast(F32)
+            for w in range(4):
+                nc.tensor.transpose(bank[:, w, :], words[:, P * w:P * (w + 1)], ident[:])
+
+        def evac_words(on_vector, dst, bank):
+            src = bank[:].rearrange("p (c h) r -> p c r h", h=2)
+            if on_vector:
+                nc.vector.tensor_copy(out=dst, in_=src)
+            else:
+                nc.scalar.copy(out=dst, in_=src)
+
+        def quantise(codes, scales, grp):
+            nc.vector.quantize_mx(out=codes.bitcast(FP8X4), scales=scales, in_=grp)
+
+        def cols(k):
+            return slice(k * P, (k + 1) * P)
+
+        def prep_w(z, bank_ids):
+            for u in range(4):
+                transposes(banks[bank_ids[u]], w_raw[z][u // 2][:, u % 2, :])
+            for u in range(4):
+                evac_words(u % 2 == 0, w_grp[z][u // 2][:].bitcast(F32)[:, u % 2], banks[bank_ids[u]])
+            for h in range(2):
+                quantise(w_codes[z][:, 4 * h * P:4 * (h + 1) * P], w_scales[z][:, 4 * h * P:4 * (h + 1) * P],
+                         w_grp[z][h][:].rearrange("p u c r t -> p (u c r t)"))
+
+        def x_transposes(pair, bank_ids):
+            for fi in range(2):
+                k, i = frame_src[2 * pair + fi]
+                transposes(banks[bank_ids[fi]], x_raw[k][:, i, :])
+
+        def x_evac(pair, bank_ids, second_on_vector):
+            view = x_grp[pair % 2][:].bitcast(F32)
+            evac_words(True, view[:, 0], banks[bank_ids[0]])
+            evac_words(second_on_vector, view[:, 1], banks[bank_ids[1]])
+
+        def x_quantise(pair):
+            s = pair % 2
+            quantise(x_codes[s][:], x_scales[s][:], x_grp[s][:].rearrange("p f c r t -> p (f c r t)"))
+
+        def stage1(pair):
+            s = pair % 2
+            for fi in range(2):
+                for z in range(2):
+                    bank = banks[2 + 2 * fi + z]
+                    for u in range(4):
+                        for c in range(2):
+                            nc.tensor.matmul_mx(
+                                out=bank[:, u, :],
+                                lhsT=w_codes[z][:, cols(2 * u + c)].bitcast(FP8X4),
+                                lhsT_scale=w_scales[z][:, cols(2 * u + c)],
+                                rhs=x_codes[s][:, cols(2 * fi + c)].bitcast(FP8X4),
+                                rhs_scale=x_scales[s][:, cols(2 * fi + c)],
+                                start=(c == 0),
+                                stop=(c == 1),
+                            )
+                    nc.scalar.copy(out=h_grp[s][:, fi, z], in_=bank[:].rearrange("p u r -> p r u"))
+
+        def h_quantise(pair):
+            quantise(ha_codes[pair % 4][:], ha_scales[pair % 4][:],
+                     h_grp[pair % 2][:].rearrange("p f z r u -> p (f z r u)"))
+
+        def h_moves(pair):
+            b, t0 = pair // 4, 2 * (pair % 4)
+            for (src_t, dst_t, j) in ((ha_codes[pair % 4], hb_codes[b % 2], 16), (ha_scales[pair % 4], hb_scales[b % 2], 4)):
+                src = src_t[:].bitcast(I32).rearrange("p (f z g j) -> p z g f j", f=2, z=2, g=8, j=j)
+                dst = dst_t[:].bitcast(I32).rearrange("p (z g t j) -> p z g t j", z=2, g=8, t=T, j=j)
+                nc.vector.tensor_copy(out=dst[:, :, :, t0:t0 + 2, :], in_=src)
+
+        def sw_quad(q, bank):
+            for k in range(4):
+                pair, fi = 2 * q + k // 2, k % 2
+                s = pair % 4
+                nc.tensor.matmul_mx(
+                    out=bank[:, k, :],
+                    lhsT=ha_codes[s][:, cols(2 * fi)].bitcast(FP8X4),
+                    lhsT_scale=ha_scales[s][:, cols(2 * fi)],
+                    rhs=ha_codes[s][:, cols(2 * fi + 1)].bitcast(FP8X4),
+                    rhs_scale=ha_scales[s][:, cols(2 * fi + 1)],
+                    start=True,
+                    stop=True,
+                )
+            nc.scalar.mul(out=sw_sb[q % 3][:], in_=bank[:], mul=1.0 / N)
+            nc.sync.dma_start(out=swf[:, 4 * q:4 * q + 4, :], in_=sw_sb[q % 3][:])
+
+        def tw_passes(b, half, bank):
+            s = b % 2
+            for gg in range(4):
+                g = 4 * half + gg
+                nc.tensor.matmul_mx(
+                    out=bank[:, gg, :],
+                    lhsT=hb_codes[s][:, cols(g)].bitcast(FP8X4),
+                    lhsT_scale=hb_scales[s][:, cols(g)],
+                    rhs=hb_codes[s][:, cols(8 + g)].bitcast(FP8X4),
+                    rhs_scale=hb_scales[s][:, cols(8 + g)],
+                    start=True,
+                    stop=True,
+                )
+
+        def tw_post(b, half, bank):
+            tmp = tw_tmp[half]
+            nc.vector.tensor_tensor(out=tmp[:], in0=bank[:].rearrange("p g (s j) -> p (g s) j", j=16),
+                                    in1=m16[:].unsqueeze(1).to_broadcast([P, 32, 16]), op=ALU.mult)
+            nc.vector.tensor_reduce(out=tw_res[:, b, 32 * half:32 * half + 32], in_=tmp[:],
+                                    axis=mybir.AxisListType.X, op=ALU.add)
+            if half == 1:
+                for t in range(T):
+                    nc.sync.dma_start(out=out_1[b, t].rearrange("(g j) s -> j g s", j=16),
+                                      in_=tw_res[16 * t:16 * t + 16, b, :].rearrange("p (g s) -> p g s", s=T))
+
+        prep_w(0, (0, 1, 2, 3))
+        x_transposes(0, (4, 5))
+        x_evac(0, (4, 5), False)
+        x_quantise(0)
+        prep_w(1, (6, 7, 2, 3))
+
+        ring = [6, 7]
+        uses = 0
+        pending = []
+        for i in range(PAIRS + 2):
+            if i + 1 < PAIRS:
+                x_transposes(i + 1, (0, 1))
+            if 1 <= i <= PAIRS:
+                h_quantise(i - 1)
+            if i + 1 < PAIRS:
+                x_evac(i + 1, (0, 1), i % 2 == 0)
+            if 1 <= i <= PAIRS:
+                h_moves(i - 1)
+            if i + 1 < PAIRS:
+                x_quantise(i + 1)
+            for job in pending:
+                tw_post(*job)
+            pending = []
+            if i < PAIRS:
+                stage1(i)
+            if 1 <= i <= PAIRS and (i - 1) % 2 == 1:
+                sw_quad((i - 1) // 2, banks[ring[uses % 2]])
+                uses += 1
+            if 1 <= i <= PAIRS and (i - 1) % 4 == 3:
+                b = (i - 1) // 4
+                tw_passes(b, 0, banks[ring[uses % 2]])
+                pending.append((b, 0, banks[ring[uses % 2]]))
+                uses += 1
+            if 2 <= i and (i - 2) % 4 == 3:
+                b = (i - 2) // 4
+                tw_passes(b, 1, banks[ring[uses % 2]])
+                pending.append((b, 1, banks[ring[uses % 2]]))
+                uses += 1
+        for job in pending:
+            tw_post(*job)

@@ -10,11 +10,14 @@ I32 = mybir.dt.int32
 U8 = mybir.dt.uint8
 FP8X4 = mybir.dt.float8_e4m3fn_x4
 ALU = mybir.AluOpType
+AX = mybir.AxisListType
 
 P = 128
 B, T, N, D, L = 4, 8, 128, 1024, 512
 FRAMES = B * T
-PAIRS = FRAMES // 2
+QUADS = FRAMES // 4
+HA = 8
+LATE = 2
 FLOPS = 2 * 2 * FRAMES * N * D * L + 2 * FRAMES * N * N * L + 2 * B * N * T * T * L
 
 
@@ -39,23 +42,22 @@ def tile_higcin_volleyball_pa_t_kernel(tc, x, Wtheta, Wphi, out_0, out_1):
         m16raw = keep.tile([P, 16], F32, name="m16raw")
         m16 = keep.tile([P, 16], F32, name="m16")
 
-        w_grp = [[keep.tile([P, 2, 2, P, 4], BF16, name="w_grp%d%d" % (z, h), align_bytes=64) for h in range(2)]
-                 for z in range(2)]
+        w_grp = [keep.tile([P, 4, 2, P, 4], BF16, name="w_grp%d" % z, align_bytes=64) for z in range(2)]
         w_codes = [keep.tile([P, 8 * P], U32, name="w_codes%d" % z, align_bytes=64) for z in range(2)]
         w_scales = [keep.tile([P, 8 * P], U8, name="w_scales%d" % z, align_bytes=64) for z in range(2)]
 
-        x_grp = [keep.tile([P, 2, 2, P, 4], BF16, name="x_grp%d" % k, align_bytes=64) for k in range(2)]
-        x_codes = [keep.tile([P, 4 * P], U32, name="x_codes%d" % k, align_bytes=64) for k in range(2)]
-        x_scales = [keep.tile([P, 4 * P], U8, name="x_scales%d" % k, align_bytes=64) for k in range(2)]
+        x_grp = [keep.tile([P, 4, 2, P, 4], BF16, name="x_grp%d" % k, align_bytes=64) for k in range(2)]
+        x_codes = [keep.tile([P, 8 * P], U32, name="x_codes%d" % k, align_bytes=64) for k in range(2)]
+        x_scales = [keep.tile([P, 8 * P], U8, name="x_scales%d" % k, align_bytes=64) for k in range(2)]
 
-        h_grp = [keep.tile([P, 2, 2, P, 4], BF16, name="h_grp%d" % k, align_bytes=64) for k in range(2)]
-        ha_codes = [keep.tile([P, 4 * P], U32, name="ha_codes%d" % k, align_bytes=64) for k in range(4)]
-        ha_scales = [keep.tile([P, 4 * P], U8, name="ha_scales%d" % k, align_bytes=64) for k in range(4)]
+        h_grp = [keep.tile([P, 2, 2, P, 4], BF16, name="h_grp%d" % k, align_bytes=64) for k in range(3)]
+        ha_codes = [keep.tile([P, 4 * P], U32, name="ha_codes%d" % k, align_bytes=64) for k in range(HA)]
+        ha_scales = [keep.tile([P, 4 * P], U8, name="ha_scales%d" % k, align_bytes=64) for k in range(HA)]
         hb_codes = [keep.tile([P, 16 * P], U32, name="hb_codes%d" % k, align_bytes=64) for k in range(2)]
         hb_scales = [keep.tile([P, 16 * P], U8, name="hb_scales%d" % k, align_bytes=64) for k in range(2)]
 
         sw_sb = [keep.tile([P, 4, P], F32, name="sw_sb%d" % k) for k in range(3)]
-        tw_tmp = [keep.tile([P, 32, 16], F32, name="tw_tmp%d" % k) for k in range(2)]
+        tw_tmp = [keep.tile([P, 64, 16], F32, name="tw_tmp%d" % k) for k in range(2)]
         tw_res = keep.tile([P, B, 64], F32, name="tw_res")
 
         xf = x.rearrange("b t j d -> j (b t) d")
@@ -72,102 +74,87 @@ def tile_higcin_volleyball_pa_t_kernel(tc, x, Wtheta, Wphi, out_0, out_1):
 
         load_w(0)
         load_x(0)
+        load_x(1)
         load_w(1)
-        for k in range(1, len(chunks)):
+        for k in range(2, len(chunks)):
             load_x(k)
 
         masks.make_identity(nc, ident[:])
-        for k in range(4):
+        for k in range(HA):
             nc.vector.memset(ha_scales[k][:].bitcast(I32), 0)
-        nc.vector.tensor_reduce(out=m16raw[:], in_=ident[:].rearrange("p (t j) -> p j t", j=16),
-                                axis=mybir.AxisListType.X, op=ALU.add)
+        nc.vector.tensor_reduce(out=m16raw[:], in_=ident[:].rearrange("p (t j) -> p j t", j=16), axis=AX.X, op=ALU.add)
         nc.vector.tensor_scalar_mul(out=m16[:], in0=m16raw[:], scalar1=1.0 / T)
+
+        def cols(k, n=1):
+            return slice(k * P, (k + n) * P)
 
         def transposes(bank, src):
             words = src.bitcast(F32)
             for w in range(4):
-                nc.tensor.transpose(bank[:, w, :], words[:, P * w:P * (w + 1)], ident[:])
+                nc.tensor.transpose(bank[:, w, :], words[:, cols(w)], ident[:])
 
-        def evac_words(on_vector, dst, bank):
-            src = bank[:].rearrange("p (c h) r -> p c r h", h=2)
+        def copy_out(on_vector, dst, src):
             if on_vector:
                 nc.vector.tensor_copy(out=dst, in_=src)
             else:
                 nc.scalar.copy(out=dst, in_=src)
 
-        def quantise(codes, scales, grp):
-            nc.vector.quantize_mx(out=codes.bitcast(FP8X4), scales=scales, in_=grp)
+        def evac_words(on_vector, grp, unit, bank):
+            copy_out(on_vector, grp[:].bitcast(F32)[:, unit], bank[:].rearrange("p (c h) r -> p c r h", h=2))
 
-        def cols(k):
-            return slice(k * P, (k + 1) * P)
+        def quantise(codes, scales, grp, first, count):
+            flat = grp[:].rearrange("p a b r t -> p (a b r t)")
+            nc.vector.quantize_mx(out=codes[:, cols(first, count)].bitcast(FP8X4), scales=scales[:, cols(first, count)],
+                                  in_=flat[:, 4 * P * first:4 * P * (first + count)])
 
-        def prep_w(z, bank_ids):
+        def w_transposes(z, ids):
             for u in range(4):
-                transposes(banks[bank_ids[u]], w_raw[z][u // 2][:, u % 2, :])
+                transposes(banks[ids[u]], w_raw[z][u // 2][:, u % 2, :])
+
+        def x_transposes(f, bank):
+            k, i = frame_src[f]
+            transposes(bank, x_raw[k][:, i, :])
+
+        def stage1(f, z, bank, on_vector):
+            s = (f // 4) % 2
             for u in range(4):
-                evac_words(u % 2 == 0, w_grp[z][u // 2][:].bitcast(F32)[:, u % 2], banks[bank_ids[u]])
-            for h in range(2):
-                quantise(w_codes[z][:, 4 * h * P:4 * (h + 1) * P], w_scales[z][:, 4 * h * P:4 * (h + 1) * P],
-                         w_grp[z][h][:].rearrange("p u c r t -> p (u c r t)"))
+                for c in range(2):
+                    nc.tensor.matmul_mx(
+                        out=bank[:, u, :],
+                        lhsT=w_codes[z][:, cols(2 * u + c)].bitcast(FP8X4),
+                        lhsT_scale=w_scales[z][:, cols(2 * u + c)],
+                        rhs=x_codes[s][:, cols(2 * (f % 4) + c)].bitcast(FP8X4),
+                        rhs_scale=x_scales[s][:, cols(2 * (f % 4) + c)],
+                        start=(c == 0),
+                        stop=(c == 1),
+                    )
+            copy_out(on_vector, h_grp[(f // 2) % 3][:, f % 2, z], bank[:].rearrange("p u r -> p r u"))
 
-        def x_transposes(pair, bank_ids):
-            for fi in range(2):
-                k, i = frame_src[2 * pair + fi]
-                transposes(banks[bank_ids[fi]], x_raw[k][:, i, :])
+        def h_quantise(pair, first=0, count=4):
+            quantise(ha_codes[pair % HA], ha_scales[pair % HA], h_grp[pair % 3], first, count)
 
-        def x_evac(pair, bank_ids, second_on_vector):
-            view = x_grp[pair % 2][:].bitcast(F32)
-            evac_words(True, view[:, 0], banks[bank_ids[0]])
-            evac_words(second_on_vector, view[:, 1], banks[bank_ids[1]])
-
-        def x_quantise(pair):
-            s = pair % 2
-            quantise(x_codes[s][:], x_scales[s][:], x_grp[s][:].rearrange("p f c r t -> p (f c r t)"))
-
-        def stage1(pair):
-            s = pair % 2
-            for fi in range(2):
-                for z in range(2):
-                    bank = banks[2 + 2 * fi + z]
-                    for u in range(4):
-                        for c in range(2):
-                            nc.tensor.matmul_mx(
-                                out=bank[:, u, :],
-                                lhsT=w_codes[z][:, cols(2 * u + c)].bitcast(FP8X4),
-                                lhsT_scale=w_scales[z][:, cols(2 * u + c)],
-                                rhs=x_codes[s][:, cols(2 * fi + c)].bitcast(FP8X4),
-                                rhs_scale=x_scales[s][:, cols(2 * fi + c)],
-                                start=(c == 0),
-                                stop=(c == 1),
-                            )
-                    nc.scalar.copy(out=h_grp[s][:, fi, z], in_=bank[:].rearrange("p u r -> p r u"))
-
-        def h_quantise(pair):
-            quantise(ha_codes[pair % 4][:], ha_scales[pair % 4][:],
-                     h_grp[pair % 2][:].rearrange("p f z r u -> p (f z r u)"))
-
-        def h_moves(pair):
+        def h_moves(pair, f0=0, nf=2):
             b, t0 = pair // 4, 2 * (pair % 4)
-            for (src_t, dst_t, j) in ((ha_codes[pair % 4], hb_codes[b % 2], 16), (ha_scales[pair % 4], hb_scales[b % 2], 4)):
+            for (src_t, dst_t, j) in ((ha_codes[pair % HA], hb_codes[b % 2], 16), (ha_scales[pair % HA], hb_scales[b % 2], 4)):
                 src = src_t[:].bitcast(I32).rearrange("p (f z g j) -> p z g f j", f=2, z=2, g=8, j=j)
                 dst = dst_t[:].bitcast(I32).rearrange("p (z g t j) -> p z g t j", z=2, g=8, t=T, j=j)
-                nc.vector.tensor_copy(out=dst[:, :, :, t0:t0 + 2, :], in_=src)
+                nc.vector.tensor_copy(out=dst[:, :, :, t0 + f0:t0 + f0 + nf, :], in_=src[:, :, :, f0:f0 + nf, :])
 
-        def sw_quad(q, bank):
-            for k in range(4):
-                pair, fi = 2 * q + k // 2, k % 2
-                s = pair % 4
-                nc.tensor.matmul_mx(
-                    out=bank[:, k, :],
-                    lhsT=ha_codes[s][:, cols(2 * fi)].bitcast(FP8X4),
-                    lhsT_scale=ha_scales[s][:, cols(2 * fi)],
-                    rhs=ha_codes[s][:, cols(2 * fi + 1)].bitcast(FP8X4),
-                    rhs_scale=ha_scales[s][:, cols(2 * fi + 1)],
-                    start=True,
-                    stop=True,
-                )
+        def sw_pass(f, bank):
+            s, fi = (f // 2) % HA, f % 2
+            nc.tensor.matmul_mx(
+                out=bank[:, f % 4, :],
+                lhsT=ha_codes[s][:, cols(2 * fi)].bitcast(FP8X4),
+                lhsT_scale=ha_scales[s][:, cols(2 * fi)],
+                rhs=ha_codes[s][:, cols(2 * fi + 1)].bitcast(FP8X4),
+                rhs_scale=ha_scales[s][:, cols(2 * fi + 1)],
+                start=True,
+                stop=True,
+            )
+
+        def sw_out(q, bank, queue):
             nc.scalar.mul(out=sw_sb[q % 3][:], in_=bank[:], mul=1.0 / N)
-            nc.sync.dma_start(out=swf[:, 4 * q:4 * q + 4, :], in_=sw_sb[q % 3][:])
+            queue.dma_start(out=swf[:, 4 * q:4 * q + 4, :], in_=sw_sb[q % 3][:])
 
         def tw_passes(b, half, bank):
             s = b % 2
@@ -183,54 +170,108 @@ def tile_higcin_volleyball_pa_t_kernel(tc, x, Wtheta, Wphi, out_0, out_1):
                     stop=True,
                 )
 
-        def tw_post(b, half, bank):
-            tmp = tw_tmp[half]
-            nc.vector.tensor_tensor(out=tmp[:], in0=bank[:].rearrange("p g (s j) -> p (g s) j", j=16),
+        def tw_mask(b, half, bank):
+            nc.vector.tensor_tensor(out=tw_tmp[b % 2][:, 32 * half:32 * half + 32, :],
+                                    in0=bank[:].rearrange("p g (s j) -> p (g s) j", j=16),
                                     in1=m16[:].unsqueeze(1).to_broadcast([P, 32, 16]), op=ALU.mult)
-            nc.vector.tensor_reduce(out=tw_res[:, b, 32 * half:32 * half + 32], in_=tmp[:],
-                                    axis=mybir.AxisListType.X, op=ALU.add)
-            if half == 1:
-                for t in range(T):
-                    nc.sync.dma_start(out=out_1[b, t].rearrange("(g j) s -> j g s", j=16),
-                                      in_=tw_res[16 * t:16 * t + 16, b, :].rearrange("p (g s) -> p g s", s=T))
 
-        prep_w(0, (0, 1, 2, 3))
-        x_transposes(0, (4, 5))
-        x_evac(0, (4, 5), False)
-        x_quantise(0)
-        prep_w(1, (6, 7, 2, 3))
+        def tw_out(b, queues):
+            nc.vector.tensor_reduce(out=tw_res[:, b, :], in_=tw_tmp[b % 2][:], axis=AX.X, op=ALU.add)
+            for t in range(T):
+                queues[t % len(queues)].dma_start(out=out_1[b, t].rearrange("(g j) s -> j g s", j=16),
+                                                  in_=tw_res[16 * t:16 * t + 16, b, :].rearrange("p (g s) -> p g s", s=T))
 
-        ring = [6, 7]
-        uses = 0
-        pending = []
-        for i in range(PAIRS + 2):
-            if i + 1 < PAIRS:
-                x_transposes(i + 1, (0, 1))
-            if 1 <= i <= PAIRS:
-                h_quantise(i - 1)
-            if i + 1 < PAIRS:
-                x_evac(i + 1, (0, 1), i % 2 == 0)
-            if 1 <= i <= PAIRS:
-                h_moves(i - 1)
-            if i + 1 < PAIRS:
-                x_quantise(i + 1)
-            for job in pending:
-                tw_post(*job)
-            pending = []
-            if i < PAIRS:
-                stage1(i)
-            if 1 <= i <= PAIRS and (i - 1) % 2 == 1:
-                sw_quad((i - 1) // 2, banks[ring[uses % 2]])
-                uses += 1
-            if 1 <= i <= PAIRS and (i - 1) % 4 == 3:
-                b = (i - 1) // 4
-                tw_passes(b, 0, banks[ring[uses % 2]])
-                pending.append((b, 0, banks[ring[uses % 2]]))
-                uses += 1
-            if 2 <= i and (i - 2) % 4 == 3:
-                b = (i - 2) // 4
-                tw_passes(b, 1, banks[ring[uses % 2]])
-                pending.append((b, 1, banks[ring[uses % 2]]))
-                uses += 1
-        for job in pending:
-            tw_post(*job)
+        w_transposes(0, (0, 1, 2, 3))
+        for u in range(4):
+            evac_words(u % 2 == 0, w_grp[0], u, banks[u])
+            if u % 2 == 1:
+                quantise(w_codes[0], w_scales[0], w_grp[0], 4 * (u // 2), 4)
+        for f in range(4):
+            x_transposes(f, banks[4 + f])
+        for f in range(2):
+            evac_words(False, x_grp[0], f, banks[4 + f])
+            quantise(x_codes[0], x_scales[0], x_grp[0], 2 * f, 2)
+        evac_words(True, x_grp[0], 2, banks[6])
+        evac_words(False, x_grp[0], 3, banks[7])
+        quantise(x_codes[0], x_scales[0], x_grp[0], 4, 4)
+        stage1(0, 0, banks[0], False)
+        stage1(1, 0, banks[1], False)
+        w_transposes(1, (4, 5, 6, 7))
+        evac_words(True, w_grp[1], 0, banks[4])
+        evac_words(False, w_grp[1], 1, banks[5])
+        quantise(w_codes[1], w_scales[1], w_grp[1], 0, 4)
+        evac_words(False, w_grp[1], 2, banks[6])
+        evac_words(True, w_grp[1], 3, banks[7])
+        quantise(w_codes[1], w_scales[1], w_grp[1], 4, 4)
+        stage1(2, 0, banks[2], False)
+        stage1(3, 0, banks[3], False)
+        for f in range(4, 8):
+            x_transposes(f, banks[f - 4])
+        for f in range(4):
+            evac_words(f % 2 == 0, x_grp[1], f, banks[f])
+        quantise(x_codes[1], x_scales[1], x_grp[1], 0, 4)
+        quantise(x_codes[1], x_scales[1], x_grp[1], 4, 4)
+        for f in range(4):
+            stage1(f, 1, banks[4 + f], False)
+        h_quantise(0)
+        h_moves(0)
+
+        LASTQ = QUADS - 1
+        for J in range(1, QUADS):
+            nxt = J + 1
+            s = nxt % 2
+            more = nxt < QUADS
+            if more:
+                for i in range(4):
+                    x_transposes(4 * nxt + i, banks[i])
+                evac_words(True, x_grp[s], 0, banks[0])
+            h_quantise(2 * J - 1)
+            if more:
+                evac_words(True, x_grp[s], 1, banks[1])
+            h_moves(2 * J - 1)
+            if more:
+                evac_words(False, x_grp[s], 2, banks[2])
+                evac_words(False, x_grp[s], 3, banks[3])
+                quantise(x_codes[s], x_scales[s], x_grp[s], 0, 4)
+                quantise(x_codes[s], x_scales[s], x_grp[s], 4, 4)
+            for k in range(4):
+                stage1(4 * J + k // 2, k % 2, banks[4 + k], False)
+            if J - 1 < QUADS - 1 - LATE:
+                for f in range(4 * J - 4, 4 * J):
+                    sw_pass(f, banks[0])
+                sw_out(J - 1, banks[0], nc.sync)
+            b = (J - 1) // 2
+            if (J - 1) % 2 == 1:
+                for half in range(2):
+                    tw_passes(b, half, banks[1 + half])
+                    tw_mask(b, half, banks[1 + half])
+            if J < LASTQ:
+                for k in range(4):
+                    stage1(4 * J + 2 + k // 2, k % 2, banks[4 + k], False)
+                h_quantise(2 * J)
+                if (J - 1) % 2 == 1:
+                    tw_out(b, [nc.sync])
+                h_moves(2 * J)
+            else:
+                h_quantise(2 * J)
+                h_moves(2 * J)
+                for fi in range(2):
+                    f = 4 * J + 2 + fi
+                    stage1(f, 0, banks[4 + 2 * fi], False)
+                    stage1(f, 1, banks[5 + 2 * fi], True)
+                    h_quantise(2 * J + 1, 2 * fi, 2)
+                for fi in range(2):
+                    h_moves(2 * J + 1, fi, 1)
+
+        for q in range(QUADS - 1 - LATE, QUADS - 1):
+            k = q - (QUADS - 1 - LATE)
+            for f in range(4 * q, 4 * q + 4):
+                sw_pass(f, banks[k])
+            sw_out(q, banks[k], nc.sync)
+        for f in range(FRAMES - 4, FRAMES):
+            sw_pass(f, banks[3])
+        for half in range(2):
+            tw_passes(B - 1, half, banks[4 + half])
+            tw_mask(B - 1, half, banks[4 + half])
+        sw_out(QUADS - 1, banks[3], nc.gpsimd)
+        tw_out(B - 1, [nc.sync, nc.scalar])

@@ -268,10 +268,15 @@ def tile_higcin_volleyball_pa_t_kernel(tc, x, Wtheta, Wphi, out_0, out_1):
             for f in range(4 * q, 4 * q + 4):
                 sw_pass(f, banks[k])
             sw_out(q, banks[k], nc.sync)
-        for f in range(FRAMES - 4, FRAMES):
+        for f in range(FRAMES - 4, FRAMES - 1):
             sw_pass(f, banks[3])
+        last = sw_sb[(QUADS - 1) % 3]
+        nc.scalar.mul(out=last[:, 0:3, :], in_=banks[3][:, 0:3, :], mul=1.0 / N)
+        nc.sync.dma_start(out=swf[:, FRAMES - 4:FRAMES - 1, :], in_=last[:, 0:3, :])
+        sw_pass(FRAMES - 1, banks[2])
         for half in range(2):
             tw_passes(B - 1, half, banks[4 + half])
             tw_mask(B - 1, half, banks[4 + half])
-        sw_out(QUADS - 1, banks[3], nc.gpsimd)
+        nc.scalar.mul(out=last[:, 3, :], in_=banks[2][:, 3, :], mul=1.0 / N)
+        nc.gpsimd.dma_start(out=swf[:, FRAMES - 1, :], in_=last[:, 3, :])
         tw_out(B - 1, [nc.sync, nc.scalar])

@@ -17,7 +17,7 @@ B, T, N, D, L = 4, 8, 128, 1024, 512
 FRAMES = B * T
 QUADS = FRAMES // 4
 HA = 8
-LATE = 2
+LATE = 3
 FLOPS = 2 * 2 * FRAMES * N * D * L + 2 * FRAMES * N * N * L + 2 * B * N * T * T * L
 
 
@@ -31,7 +31,7 @@ def tile_higcin_volleyball_pa_t_kernel(tc, x, Wtheta, Wphi, out_0, out_1):
         banks = [psum.tile([P, 4, P], F32, name="bank%d" % k) for k in range(8)]
 
         w_raw = [[keep.tile([P, 2, D], BF16, name="w_raw%d%d" % (z, h)) for h in range(2)] for z in range(2)]
-        chunks = [(0, 2), (2, 2)] + [(f, 4) for f in range(4, FRAMES, 4)]
+        chunks = [(0, 1), (1, 1), (2, 1), (3, 1), (4, 2), (6, 2)] + [(f, 4) for f in range(8, FRAMES, 4)]
         x_raw = [keep.tile([P, n, D], BF16, name="x_raw%d" % f0) for (f0, n) in chunks]
         frame_src = {}
         for k, (f0, n) in enumerate(chunks):
@@ -56,7 +56,7 @@ def tile_higcin_volleyball_pa_t_kernel(tc, x, Wtheta, Wphi, out_0, out_1):
         hb_codes = [keep.tile([P, 16 * P], U32, name="hb_codes%d" % k, align_bytes=64) for k in range(2)]
         hb_scales = [keep.tile([P, 16 * P], U8, name="hb_scales%d" % k, align_bytes=64) for k in range(2)]
 
-        sw_sb = [keep.tile([P, 4, P], F32, name="sw_sb%d" % k) for k in range(3)]
+        sw_sb = [keep.tile([P, 4, P], F32, name="sw_sb%d" % k) for k in range(4)]
         tw_tmp = [keep.tile([P, 64, 16], F32, name="tw_tmp%d" % k) for k in range(2)]
         tw_res = keep.tile([P, B, 64], F32, name="tw_res")
 
@@ -73,10 +73,10 @@ def tile_higcin_volleyball_pa_t_kernel(tc, x, Wtheta, Wphi, out_0, out_1):
             nc.sync.dma_start(out=x_raw[k][:], in_=xf[:, f0:f0 + n, :])
 
         load_w(0)
-        load_x(0)
-        load_x(1)
+        for k in range(4):
+            load_x(k)
         load_w(1)
-        for k in range(2, len(chunks)):
+        for k in range(4, len(chunks)):
             load_x(k)
 
         masks.make_identity(nc, ident[:])
@@ -153,8 +153,8 @@ def tile_higcin_volleyball_pa_t_kernel(tc, x, Wtheta, Wphi, out_0, out_1):
             )
 
         def sw_out(q, bank, queue):
-            nc.scalar.mul(out=sw_sb[q % 3][:], in_=bank[:], mul=1.0 / N)
-            queue.dma_start(out=swf[:, 4 * q:4 * q + 4, :], in_=sw_sb[q % 3][:])
+            nc.scalar.mul(out=sw_sb[q % 4][:], in_=bank[:], mul=1.0 / N)
+            queue.dma_start(out=swf[:, 4 * q:4 * q + 4, :], in_=sw_sb[q % 4][:])
 
         def tw_passes(b, half, bank):
             s = b % 2
@@ -230,7 +230,7 @@ def tile_higcin_volleyball_pa_t_kernel(tc, x, Wtheta, Wphi, out_0, out_1):
                 evac_words(True, x_grp[s], 1, banks[1])
             h_moves(2 * J - 1)
             if more:
-                evac_words(False, x_grp[s], 2, banks[2])
+                evac_words(J % 2 == 1, x_grp[s], 2, banks[2])
                 evac_words(False, x_grp[s], 3, banks[3])
                 quantise(x_codes[s], x_scales[s], x_grp[s], 0, 4)
                 quantise(x_codes[s], x_scales[s], x_grp[s], 4, 4)
@@ -258,7 +258,7 @@ def tile_higcin_volleyball_pa_t_kernel(tc, x, Wtheta, Wphi, out_0, out_1):
                 for fi in range(2):
                     f = 4 * J + 2 + fi
                     stage1(f, 0, banks[4 + 2 * fi], False)
-                    stage1(f, 1, banks[5 + 2 * fi], True)
+                    stage1(f, 1, banks[5 + 2 * fi], fi == 1)
                     h_quantise(2 * J + 1, 2 * fi, 2)
                 for fi in range(2):
                     h_moves(2 * J + 1, fi, 1)
@@ -268,15 +268,10 @@ def tile_higcin_volleyball_pa_t_kernel(tc, x, Wtheta, Wphi, out_0, out_1):
             for f in range(4 * q, 4 * q + 4):
                 sw_pass(f, banks[k])
             sw_out(q, banks[k], nc.sync)
-        for f in range(FRAMES - 4, FRAMES - 1):
+        for f in range(FRAMES - 4, FRAMES):
             sw_pass(f, banks[3])
-        last = sw_sb[(QUADS - 1) % 3]
-        nc.scalar.mul(out=last[:, 0:3, :], in_=banks[3][:, 0:3, :], mul=1.0 / N)
-        nc.sync.dma_start(out=swf[:, FRAMES - 4:FRAMES - 1, :], in_=last[:, 0:3, :])
-        sw_pass(FRAMES - 1, banks[2])
         for half in range(2):
             tw_passes(B - 1, half, banks[4 + half])
             tw_mask(B - 1, half, banks[4 + half])
-        nc.scalar.mul(out=last[:, 3, :], in_=banks[2][:, 3, :], mul=1.0 / N)
-        nc.gpsimd.dma_start(out=swf[:, FRAMES - 1, :], in_=last[:, 3, :])
+        sw_out(QUADS - 1, banks[3], nc.gpsimd)
         tw_out(B - 1, [nc.sync, nc.scalar])

@@ -134,11 +134,14 @@ def tile_higcin_volleyball_pa_t_kernel(tc, x, Wtheta, Wphi, out_0, out_1):
             quantise(ha_codes[pair % HA], ha_scales[pair % HA], h_grp[pair % 3], first, count)
 
         def h_moves(pair, f0=0, nf=2):
-            b, t0 = pair // 4, 2 * (pair % 4)
-            for (src_t, dst_t, j) in ((ha_codes[pair % HA], hb_codes[b % 2], 16), (ha_scales[pair % HA], hb_scales[b % 2], 4)):
-                src = src_t[:].bitcast(I32).rearrange("p (f z g j) -> p z g f j", f=2, z=2, g=8, j=j)
-                dst = dst_t[:].bitcast(I32).rearrange("p (z g t j) -> p z g t j", z=2, g=8, t=T, j=j)
-                nc.vector.tensor_copy(out=dst[:, :, :, t0 + f0:t0 + f0 + nf, :], in_=src[:, :, :, f0:f0 + nf, :])
+            b, t0 = pair // 4, 2 * (pair % 4) + f0
+            src = ha_codes[pair % HA][:].bitcast(I32).rearrange("p (f z a g c) -> p z g f a c", f=2, z=2, a=4, g=8)
+            dst = hb_codes[b % 2][:].bitcast(I32).rearrange("p (z g t a c) -> p z g t a c", z=2, g=8, t=T, a=4)
+            for z in range(2):
+                nc.vector.tensor_copy(out=dst[:, z, :, t0:t0 + nf], in_=src[:, z, :, f0:f0 + nf])
+            src = ha_scales[pair % HA][:].bitcast(I32).rearrange("p (f z a g) -> p z g f a", f=2, z=2, a=4)
+            dst = hb_scales[b % 2][:].bitcast(I32).rearrange("p (z g t a) -> p z g t a", z=2, g=8, t=T)
+            nc.vector.tensor_copy(out=dst[:, :, :, t0:t0 + nf], in_=src[:, :, :, f0:f0 + nf])
 
         def sw_pass(f, bank):
             s, fi = (f // 2) % HA, f % 2
@@ -177,9 +180,9 @@ def tile_higcin_volleyball_pa_t_kernel(tc, x, Wtheta, Wphi, out_0, out_1):
 
         def tw_out(b, queues):
             nc.vector.tensor_reduce(out=tw_res[:, b, :], in_=tw_tmp[b % 2][:], axis=AX.X, op=ALU.add)
-            for t in range(T):
-                queues[t % len(queues)].dma_start(out=out_1[b, t].rearrange("(g j) s -> j g s", j=16),
-                                                  in_=tw_res[16 * t:16 * t + 16, b, :].rearrange("p (g s) -> p g s", s=T))
+            rows = out_1[b].rearrange("t (a g c) s -> c (t a) g s", a=4, g=8)
+            for c in range(4):
+                queues[c % len(queues)].dma_start(out=rows[c], in_=tw_res[c:P:4, b, :].rearrange("p (g s) -> p g s", s=T))
 
         w_transposes(0, (0, 1, 2, 3))
         for u in range(4):
@@ -273,5 +276,5 @@ def tile_higcin_volleyball_pa_t_kernel(tc, x, Wtheta, Wphi, out_0, out_1):
         for half in range(2):
             tw_passes(B - 1, half, banks[4 + half])
             tw_mask(B - 1, half, banks[4 + half])
-        sw_out(QUADS - 1, banks[3], nc.gpsimd)
+        sw_out(QUADS - 1, banks[3], nc.sync)
         tw_out(B - 1, [nc.sync, nc.scalar])

from contextlib import ExitStack

import concourse.masks as masks
import concourse.mybir as mybir

F32 = mybir.dt.float32
BF16 = mybir.dt.bfloat16
U32 = mybir.dt.uint32
I32 = mybir.dt.int32
U8 = mybir.dt.uint8
FP8X4 = mybir.dt.float8_e4m3fn_x4
ALU = mybir.AluOpType
AX = mybir.AxisListType

P = 128
B, T, N, D, L = 4, 8, 128, 1024, 512
FRAMES = B * T
QUADS = FRAMES // 4
HA = 8
LATE = 3
FLOPS = 2 * 2 * FRAMES * N * D * L + 2 * FRAMES * N * N * L + 2 * B * N * T * T * L


def tile_higcin_volleyball_pa_t_kernel(tc, x, Wtheta, Wphi, out_0, out_1):
    nc = tc.nc
    with ExitStack() as ctx:
        keep = ctx.enter_context(tc.tile_pool(name="keep", bufs=1))
        psum = ctx.enter_context(tc.psum_pool(name="psum", bufs=1))
        ctx.enter_context(tc.manual_schedule())

        banks = [psum.tile([P, 4, P], F32, name="bank%d" % k) for k in range(8)]

        w_raw = [[keep.tile([P, 2, D], BF16, name="w_raw%d%d" % (z, h)) for h in range(2)] for z in range(2)]
        chunks = [(0, 1), (1, 1), (2, 1), (3, 1), (4, 2), (6, 2)] + [(f, 4) for f in range(8, FRAMES, 4)]
        x_raw = [keep.tile([P, n, D], BF16, name="x_raw%d" % f0) for (f0, n) in chunks]
        frame_src = {}
        for k, (f0, n) in enumerate(chunks):
            for i in range(n):
                frame_src[f0 + i] = (k, i)

        ident = keep.tile([P, P], F32, name="ident")
        m16raw = keep.tile([P, 16], F32, name="m16raw")
        m16 = keep.tile([P, 16], F32, name="m16")

        w_grp = [keep.tile([P, 4, 2, P, 4], BF16, name="w_grp%d" % z, align_bytes=64) for z in range(2)]
        w_codes = [keep.tile([P, 8 * P], U32, name="w_codes%d" % z, align_bytes=64) for z in range(2)]
        w_scales = [keep.tile([P, 8 * P], U8, name="w_scales%d" % z, align_bytes=64) for z in range(2)]

        x_grp = [keep.tile([P, 4, 2, P, 4], BF16, name="x_grp%d" % k, align_bytes=64) for k in range(2)]
        x_codes = [keep.tile([P, 8 * P], U32, name="x_codes%d" % k, align_bytes=64) for k in range(2)]
        x_scales = [keep.tile([P, 8 * P], U8, name="x_scales%d" % k, align_bytes=64) for k in range(2)]

        h_grp = [keep.tile([P, 2, 2, P, 4], BF16, name="h_grp%d" % k, align_bytes=64) for k in range(3)]
        ha_codes = [keep.tile([P, 4 * P], U32, name="ha_codes%d" % k, align_bytes=64) for k in range(HA)]
        ha_scales = [keep.tile([P, 4 * P], U8, name="ha_scales%d" % k, align_bytes=64) for k in range(HA)]
        hb_codes = [keep.tile([P, 16 * P], U32, name="hb_codes%d" % k, align_bytes=64) for k in range(2)]
        hb_scales = [keep.tile([P, 16 * P], U8, name="hb_scales%d" % k, align_bytes=64) for k in range(2)]

        sw_sb = [keep.tile([P, 4, P], F32, name="sw_sb%d" % k) for k in range(4)]
        tw_tmp = [keep.tile([P, 64, 16], F32, name="tw_tmp%d" % k) for k in range(2)]
        tw_res = keep.tile([P, B, 64], F32, name="tw_res")

        xf = x.rearrange("b t j d -> j (b t) d")
        swf = out_0.rearrange("b t j k -> j (b t) k")
        w_dram = [w.rearrange("(p u) d -> p u d", u=4) for w in (Wtheta, Wphi)]

        def load_w(z):
            for h in range(2):
                nc.sync.dma_start(out=w_raw[z][h][:], in_=w_dram[z][:, 2 * h:2 * h + 2, :])

        def load_x(k):
            f0, n = chunks[k]
            nc.sync.dma_start(out=x_raw[k][:], in_=xf[:, f0:f0 + n, :])

        load_w(0)
        for k in range(4):
            load_x(k)
        load_w(1)
        for k in range(4, len(chunks)):
            load_x(k)

        masks.make_identity(nc, ident[:])
        for k in range(HA):
            nc.vector.memset(ha_scales[k][:].bitcast(I32), 0)
        nc.vector.tensor_reduce(out=m16raw[:], in_=ident[:].rearrange("p (t j) -> p j t", j=16), axis=AX.X, op=ALU.add)
        nc.vector.tensor_scalar_mul(out=m16[:], in0=m16raw[:], scalar1=1.0 / T)

        def cols(k, n=1):
            return slice(k * P, (k + n) * P)

        def transposes(bank, src):
            words = src.bitcast(F32)
            for w in range(4):
                nc.tensor.transpose(bank[:, w, :], words[:, cols(w)], ident[:])

        def copy_out(on_vector, dst, src):
            if on_vector:
                nc.vector.tensor_copy(out=dst, in_=src)
            else:
                nc.scalar.copy(out=dst, in_=src)

        def evac_words(on_vector, grp, unit, bank):
            copy_out(on_vector, grp[:].bitcast(F32)[:, unit], bank[:].rearrange("p (c h) r -> p c r h", h=2))

        def quantise(codes, scales, grp, first, count):
            flat = grp[:].rearrange("p a b r t -> p (a b r t)")
            nc.vector.quantize_mx(out=codes[:, cols(first, count)].bitcast(FP8X4), scales=scales[:, cols(first, count)],
                                  in_=flat[:, 4 * P * first:4 * P * (first + count)])

        def w_transposes(z, ids):
            for u in range(4):
                transposes(banks[ids[u]], w_raw[z][u // 2][:, u % 2, :])

        def x_transposes(f, bank):
            k, i = frame_src[f]
            transposes(bank, x_raw[k][:, i, :])

        def stage1(f, z, bank, on_vector):
            s = (f // 4) % 2
            for u in range(4):
                for c in range(2):
                    nc.tensor.matmul_mx(
                        out=bank[:, u, :],
                        lhsT=w_codes[z][:, cols(2 * u + c)].bitcast(FP8X4),
                        lhsT_scale=w_scales[z][:, cols(2 * u + c)],
                        rhs=x_codes[s][:, cols(2 * (f % 4) + c)].bitcast(FP8X4),
                        rhs_scale=x_scales[s][:, cols(2 * (f % 4) + c)],
                        start=(c == 0),
                        stop=(c == 1),
                    )
            copy_out(on_vector, h_grp[(f // 2) % 3][:, f % 2, z], bank[:].rearrange("p u r -> p r u"))

        def h_quantise(pair, first=0, count=4):
            quantise(ha_codes[pair % HA], ha_scales[pair % HA], h_grp[pair % 3], first, count)

        def h_moves(pair, f0=0, nf=2):
            b, t0 = pair // 4, 2 * (pair % 4) + f0
            src = ha_codes[pair % HA][:].bitcast(I32).rearrange("p (f z a g c) -> p z g f a c", f=2, z=2, a=4, g=8)
            dst = hb_codes[b % 2][:].bitcast(I32).rearrange("p (z g t a c) -> p z g t a c", z=2, g=8, t=T, a=4)
            for z in range(2):
                nc.vector.tensor_copy(out=dst[:, z, :, t0:t0 + nf], in_=src[:, z, :, f0:f0 + nf])
            src = ha_scales[pair % HA][:].bitcast(I32).rearrange("p (f z a g) -> p z g f a", f=2, z=2, a=4)
            dst = hb_scales[b % 2][:].bitcast(I32).rearrange("p (z g t a) -> p z g t a", z=2, g=8, t=T)
            nc.vector.tensor_copy(out=dst[:, :, :, t0:t0 + nf], in_=src[:, :, :, f0:f0 + nf])

        def sw_pass(f, bank):
            s, fi = (f // 2) % HA, f % 2
            nc.tensor.matmul_mx(
                out=bank[:, f % 4, :],
                lhsT=ha_codes[s][:, cols(2 * fi)].bitcast(FP8X4),
                lhsT_scale=ha_scales[s][:, cols(2 * fi)],
                rhs=ha_codes[s][:, cols(2 * fi + 1)].bitcast(FP8X4),
                rhs_scale=ha_scales[s][:, cols(2 * fi + 1)],
                start=True,
                stop=True,
            )

        def sw_out(q, bank, queue):
            nc.scalar.mul(out=sw_sb[q % 4][:], in_=bank[:], mul=1.0 / N)
            queue.dma_start(out=swf[:, 4 * q:4 * q + 4, :], in_=sw_sb[q % 4][:])

        def tw_passes(b, half, bank):
            s = b % 2
            for gg in range(4):
                g = 4 * half + gg
                nc.tensor.matmul_mx(
                    out=bank[:, gg, :],
                    lhsT=hb_codes[s][:, cols(g)].bitcast(FP8X4),
                    lhsT_scale=hb_scales[s][:, cols(g)],
                    rhs=hb_codes[s][:, cols(8 + g)].bitcast(FP8X4),
                    rhs_scale=hb_scales[s][:, cols(8 + g)],
                    start=True,
                    stop=True,
                )

        def tw_mask(b, half, bank):
            nc.vector.tensor_tensor(out=tw_tmp[b % 2][:, 32 * half:32 * half + 32, :],
                                    in0=bank[:].rearrange("p g (s j) -> p (g s) j", j=16),
                                    in1=m16[:].unsqueeze(1).to_broadcast([P, 32, 16]), op=ALU.mult)

        def tw_out(b, queues):
            nc.vector.tensor_reduce(out=tw_res[:, b, :], in_=tw_tmp[b % 2][:], axis=AX.X, op=ALU.add)
            rows = out_1[b].rearrange("t (a g c) s -> c (t a) g s", a=4, g=8)
            for c in range(4):
                queues[c % len(queues)].dma_start(out=rows[c], in_=tw_res[c:P:4, b, :].rearrange("p (g s) -> p g s", s=T))

        w_transposes(0, (0, 1, 2, 3))
        for u in range(4):
            evac_words(u % 2 == 0, w_grp[0], u, banks[u])
            if u % 2 == 1:
                quantise(w_codes[0], w_scales[0], w_grp[0], 4 * (u // 2), 4)
        for f in range(4):
            x_transposes(f, banks[4 + f])
        for f in range(2):
            evac_words(False, x_grp[0], f, banks[4 + f])
            quantise(x_codes[0], x_scales[0], x_grp[0], 2 * f, 2)
        evac_words(True, x_grp[0], 2, banks[6])
        evac_words(False, x_grp[0], 3, banks[7])
        quantise(x_codes[0], x_scales[0], x_grp[0], 4, 4)
        stage1(0, 0, banks[0], False)
        stage1(1, 0, banks[1], False)
        w_transposes(1, (4, 5, 6, 7))
        evac_words(True, w_grp[1], 0, banks[4])
        evac_words(False, w_grp[1], 1, banks[5])
        quantise(w_codes[1], w_scales[1], w_grp[1], 0, 4)
        evac_words(False, w_grp[1], 2, banks[6])
        evac_words(True, w_grp[1], 3, banks[7])
        quantise(w_codes[1], w_scales[1], w_grp[1], 4, 4)
        stage1(2, 0, banks[2], False)
        stage1(3, 0, banks[3], False)
        for f in range(4, 8):
            x_transposes(f, banks[f - 4])
        for f in range(4):
            evac_words(f % 2 == 0, x_grp[1], f, banks[f])
        quantise(x_codes[1], x_scales[1], x_grp[1], 0, 4)
        quantise(x_codes[1], x_scales[1], x_grp[1], 4, 4)
        for f in range(4):
            stage1(f, 1, banks[4 + f], False)
        h_quantise(0)
        h_moves(0)

        LASTQ = QUADS - 1
        for J in range(1, QUADS):
            nxt = J + 1
            s = nxt % 2
            more = nxt < QUADS
            if more:
                for i in range(4):
                    x_transposes(4 * nxt + i, banks[i])
                evac_words(True, x_grp[s], 0, banks[0])
            h_quantise(2 * J - 1)
            if more:
                evac_words(True, x_grp[s], 1, banks[1])
            h_moves(2 * J - 1)
            if more:
                evac_words(J % 2 == 1, x_grp[s], 2, banks[2])
                evac_words(False, x_grp[s], 3, banks[3])
                quantise(x_codes[s], x_scales[s], x_grp[s], 0, 4)
                quantise(x_codes[s], x_scales[s], x_grp[s], 4, 4)
            for k in range(4):
                stage1(4 * J + k // 2, k % 2, banks[4 + k], False)
            if J - 1 < QUADS - 1 - LATE:
                for f in range(4 * J - 4, 4 * J):
                    sw_pass(f, banks[0])
                sw_out(J - 1, banks[0], nc.sync)
            b = (J - 1) // 2
            if (J - 1) % 2 == 1:
                for half in range(2):
                    tw_passes(b, half, banks[1 + half])
                    tw_mask(b, half, banks[1 + half])
            if J < LASTQ:
                for k in range(4):
                    stage1(4 * J + 2 + k // 2, k % 2, banks[4 + k], False)
                h_quantise(2 * J)
                if (J - 1) % 2 == 1:
                    tw_out(b, [nc.sync])
                h_moves(2 * J)
            else:
                h_quantise(2 * J)
                h_moves(2 * J)
                for fi in range(2):
                    f = 4 * J + 2 + fi
                    stage1(f, 0, banks[4 + 2 * fi], False)
                    stage1(f, 1, banks[5 + 2 * fi], fi == 1)
                    h_quantise(2 * J + 1, 2 * fi, 2)
                for fi in range(2):
                    h_moves(2 * J + 1, fi, 1)

        for q in range(QUADS - 1 - LATE, QUADS - 1):
            k = q - (QUADS - 1 - LATE)
            for f in range(4 * q, 4 * q + 4):
                sw_pass(f, banks[k])
            sw_out(q, banks[k], nc.sync)
        for f in range(FRAMES - 4, FRAMES):
            sw_pass(f, banks[3])
        for half in range(2):
            tw_passes(B - 1, half, banks[4 + half])
            tw_mask(B - 1, half, banks[4 + half])
        sw_out(QUADS - 1, banks[3], nc.sync)
        tw_out(B - 1, [nc.sync, nc.scalar])
